import numpy as np
import ml_dtypes


def mxq(x, axis, fmt="e4m3"):
    dtype, down = {"e4m3": (ml_dtypes.float8_e4m3fn, 7), "e5m2": (ml_dtypes.float8_e5m2, 14)}[fmt]
    v = np.moveaxis(np.asarray(x, np.float32).astype(ml_dtypes.bfloat16).astype(np.float64), axis, -1)
    blocks = v.reshape(v.shape[:-1] + (-1, 32))
    amax = np.abs(blocks).max(-1, keepdims=True)
    byte = np.maximum(np.where(amax > 0, np.frexp(amax)[1] - 1 + 127, 0) - down, 1)
    scale = np.exp2(byte - 127.0)
    codes = (blocks / scale).astype(np.float32).astype(dtype).astype(np.float64)
    return np.moveaxis((codes * scale).reshape(v.shape), -1, axis)


WIDE = False


def mx_kscale(k):
    if not WIDE:
        return np.ones(k)
    levels = np.array([10, -10, 5, -5, 0])
    a = np.random.permutation(np.resize(levels, k // 512 * 4)).reshape(k // 512, 4)
    idx = np.arange(k)
    return np.exp2(a[idx // 512, idx % 128 // 32])


BF16 = ml_dtypes.bfloat16


def bf(x):
    return np.asarray(x, np.float32).astype(BF16)


def f64(x):
    return np.asarray(x).astype(np.float64)


B, T, S, Dt, Df = 8, 1024, 256, 512, 512
EPS = 1e-6


def rmsnorm(x, w):
    return x * (1.0 / np.sqrt(np.mean(x * x, axis=-1, keepdims=True) + EPS)) * w


def setup_inputs():
    s = mx_kscale(Dt)
    t = mx_kscale(Df)
    return {"text": bf(np.random.standard_normal((B, T, Dt)) * s),
            "Wq_w": bf(np.random.standard_normal((Df, Dt)) / np.sqrt(Dt) / s[None, :]),
            "Wq_b": bf(np.random.standard_normal(Df) * 0.3),
            "qn_w": bf((1.0 + 0.1 * np.random.standard_normal(Df)) * t),
            "k_norm": bf(np.random.standard_normal((B, S, Df)) / t)}


def reference(text, Wq_w, Wq_b, qn_w, k_norm):
    q = (mxq(f64(text), 2, "e4m3") @ mxq(f64(Wq_w), 1, "e4m3").T) + f64(Wq_b)
    q = rmsnorm(q, f64(qn_w))
    scale = 1.0 / np.sqrt(Df)
    return (mxq(q, 2, "e4m3") @ mxq(f64(k_norm), 2, "e4m3").transpose(0, 2, 1)) * scale

@@ -1,0 +1,271 @@
+from contextlib import ExitStack
+import math
+
+import concourse.mybir as mybir
+from concourse.masks import make_identity
+
+F32 = mybir.dt.float32
+BF16 = mybir.dt.bfloat16
+U32 = mybir.dt.uint32
+U8 = mybir.dt.uint8
+FP8X4 = mybir.dt.float8_e4m3fn_x4
+ACT = mybir.ActivationFunctionType
+ALU = mybir.AluOpType
+
+P = 128
+PACK = 4
+BATCHES = 8
+TOKENS = 1024
+KEYS = 256
+D = 512
+EPS = 1e-6
+
+CHUNKS = D // P
+TILES_PER_BATCH = TOKENS // P
+KEY_TILES = KEYS // P
+BLOCK_TILES = 4
+BLOCK = BLOCK_TILES * P
+BLOCKS_PER_BATCH = TOKENS // BLOCK
+N_BLOCKS = BATCHES * BLOCKS_PER_BATCH
+PAIR = 2
+
+FLOPS = 2 * BATCHES * TOKENS * D * D + 2 * BATCHES * TOKENS * D * KEYS
+
+
+def tile_crossattention_pb_t_kernel(tc, text, Wq_w, Wq_b, qn_w, k_norm, out):
+    nc = tc.nc
+    with ExitStack() as ctx:
+        ctx.enter_context(tc.manual_schedule())
+        const = ctx.enter_context(tc.tile_pool(name="const", bufs=1))
+        raw = ctx.enter_context(tc.tile_pool(name="raw", bufs=4))
+        stage = ctx.enter_context(tc.tile_pool(name="stage", bufs=2))
+        deep = ctx.enter_context(tc.tile_pool(name="deep", bufs=3))
+        psum_ring = ctx.enter_context(tc.psum_pool(name="psum_ring", bufs=6))
+        psum_one = ctx.enter_context(tc.psum_pool(name="psum_one", bufs=1))
+
+        w_raw = const.tile([P, CHUNKS, D], BF16)
+        nc.sync.dma_start(
+            out=w_raw[:].rearrange("p (u e) k -> p u e k", e=2),
+            in_=Wq_w.rearrange("(u p e) k -> p u e k", u=2, e=2),
+        )
+        bias_bf = const.tile([P, CHUNKS], BF16)
+        gain_bf = const.tile([P, CHUNKS], BF16)
+        nc.scalar.dma_start(
+            out=bias_bf[:].rearrange("p (u e) -> p u e", e=2),
+            in_=Wq_b.rearrange("(u p e) -> p u e", u=2, e=2),
+        )
+        nc.scalar.dma_start(
+            out=gain_bf[:].rearrange("p (u e) -> p u e", e=2),
+            in_=qn_w.rearrange("(u p e) -> p u e", u=2, e=2),
+        )
+        ident = const.tile([P, P], F32)
+        make_identity(nc, ident[:])
+        ones = const.tile([P, 1], F32)
+        nc.vector.memset(ones[:], 1.0)
+        eps = const.tile([P, 1], F32)
+        nc.vector.memset(eps[:], EPS)
+        bias = const.tile([P, CHUNKS], F32)
+        gain = const.tile([P, CHUNKS], F32)
+        gain_bias = const.tile([P, CHUNKS], F32)
+        nc.vector.tensor_copy(out=bias[:], in_=bias_bf[:])
+        nc.vector.tensor_copy(out=gain[:], in_=gain_bf[:])
+        nc.vector.tensor_tensor(out=gain_bias[:], in0=gain[:], in1=bias[:], op=ALU.mult)
+
+        def transpose_and_quantise(rows, n_tiles, codes, scales):
+            words = rows.bitcast(F32)
+            grouped = deep.tile([P, n_tiles * P, PACK], BF16, align_bytes=64, tag="grouped%d" % n_tiles)
+            grouped_words = grouped[:].bitcast(F32)
+            for first in range(0, n_tiles, PAIR):
+                turned = psum_ring.tile([P, 2, PAIR * P], F32, tag="bank")
+                for j in range(PAIR):
+                    for u in range(2):
+                        nc.tensor.transpose(
+                            turned[:, u, j * P : (j + 1) * P],
+                            words[:, first + j, u * P : (u + 1) * P],
+                            ident[:],
+                        )
+                if (first // PAIR) % 2 == 0:
+                    nc.vector.tensor_copy(
+                        out=grouped_words[:, first * P : (first + PAIR) * P, :],
+                        in_=turned[:].rearrange("p u r -> p r u"),
+                    )
+                else:
+                    nc.scalar.copy(
+                        out=grouped_words[:, first * P : (first + PAIR) * P, :],
+                        in_=turned[:].rearrange("p u r -> p r u"),
+                    )
+            nc.vector.quantize_mx(
+                out=codes.bitcast(FP8X4),
+                scales=scales,
+                in_=grouped[:].rearrange("p r t -> p (r t)"),
+            )
+
+        w_codes = const.tile([P, D], U32, align_bytes=64)
+        w_scales = const.tile([P, D], U8, align_bytes=64)
+        x_codes = const.tile([P, N_BLOCKS, BLOCK], U32, align_bytes=64)
+        x_scales = const.tile([P, N_BLOCKS, BLOCK], U8, align_bytes=64)
+        k_codes = const.tile([P, BATCHES, KEYS], U32, align_bytes=64)
+        k_scales = const.tile([P, BATCHES, KEYS], U8, align_bytes=64)
+
+        transpose_and_quantise(w_raw[:], CHUNKS, w_codes[:], w_scales[:])
+        for b in range(BATCHES):
+            text_raw = raw.tile([P, TILES_PER_BATCH, D], BF16)
+            nc.sync.dma_start(out=text_raw[:], in_=text[b].rearrange("(p i) k -> p i k", i=TILES_PER_BATCH))
+            k_raw = raw.tile([P, KEY_TILES, D], BF16)
+            nc.sync.dma_start(out=k_raw[:], in_=k_norm[b].rearrange("(j p) d -> p j d", p=P))
+            for half in range(BLOCKS_PER_BATCH):
+                n = b * BLOCKS_PER_BATCH + half
+                transpose_and_quantise(
+                    text_raw[:, half * BLOCK_TILES : (half + 1) * BLOCK_TILES, :],
+                    BLOCK_TILES,
+                    x_codes[:, n, :],
+                    x_scales[:, n, :],
+                )
+            transpose_and_quantise(k_raw[:], KEY_TILES, k_codes[:, b, :], k_scales[:, b, :])
+
+        live = {}
+
+        def project(n):
+            banks = []
+            for c in range(CHUNKS):
+                q_ps = psum_ring.tile([P, BLOCK], F32, tag="bank")
+                nc.tensor.matmul_mx(
+                    out=q_ps[:],
+                    lhsT=w_codes[:, c * P : (c + 1) * P].bitcast(FP8X4),
+                    lhsT_scale=w_scales[:, c * P : (c + 1) * P],
+                    rhs=x_codes[:, n, :].bitcast(FP8X4),
+                    rhs_scale=x_scales[:, n, :],
+                    start=True,
+                    stop=True,
+                )
+                banks.append(q_ps)
+            live["q", n] = banks
+
+        def square(n):
+            squares = stage.tile([P, CHUNKS, BLOCK], F32)
+            halves = deep.tile([P, 2, BLOCK], F32)
+            for c in range(CHUNKS):
+                nc.scalar.activation(
+                    out=squares[:, c, :], in_=live["q", n][c][:], func=ACT.Square, bias=bias[:, c : c + 1], scale=1.0
+                )
+            for h in range(2):
+                nc.gpsimd.tensor_tensor(
+                    out=halves[:, h, :], in0=squares[:, 2 * h, :], in1=squares[:, 2 * h + 1, :], op=ALU.add
+                )
+            live["halves", n] = halves
+
+        def scale_on_vector(n):
+            scaled = deep.tile([P, CHUNKS, BLOCK], F32)
+            nc.vector.tensor_scalar(
+                out=scaled[:, CHUNKS - 1, :],
+                in0=live["q", n][CHUNKS - 1][:],
+                scalar1=gain[:, CHUNKS - 1 : CHUNKS],
+                scalar2=gain_bias[:, CHUNKS - 1 : CHUNKS],
+                op0=ALU.mult,
+                op1=ALU.add,
+            )
+            live["scaled", n] = scaled
+
+        def scale_on_scalar(n):
+            for c in range(CHUNKS - 1):
+                nc.scalar.activation(
+                    out=live["scaled", n][:, c, :],
+                    in_=live["q", n][c][:],
+                    func=ACT.Identity,
+                    bias=gain_bias[:, c : c + 1],
+                    scale=gain[:, c : c + 1],
+                )
+
+        def root_mean_square(n):
+            halves = live["halves", n]
+            sums = psum_one.tile([P, BLOCK_TILES], F32)
+            for i in range(BLOCK_TILES):
+                for h in range(2):
+                    nc.tensor.matmul(
+                        out=sums[:, i : i + 1],
+                        lhsT=halves[:, h, i * P : (i + 1) * P],
+                        rhs=ones[:],
+                        start=(h == 0),
+                        stop=(h == 1),
+                    )
+            rms = stage.tile([P, BLOCK_TILES], F32)
+            nc.scalar.activation(out=rms[:], in_=sums[:], func=ACT.Sqrt, bias=eps[:], scale=1.0 / D)
+            live["rms", n] = rms
+
+        def spread_inverse(n):
+            rstd = stage.tile([P, BLOCK_TILES], F32)
+            nc.vector.reciprocal(out=rstd[:], in_=live["rms", n][:])
+            spread = psum_one.tile([P, BLOCK], F32)
+            for i in range(BLOCK_TILES):
+                nc.tensor.transpose(
+                    spread[:, i * P : (i + 1) * P], rstd[:, i : i + 1].to_broadcast([P, P]), ident[:]
+                )
+            live["spread", n] = spread
+
+        def normalise(n):
+            q_grouped = stage.tile([P, BLOCK, PACK], BF16, align_bytes=64)
+            nc.vector.tensor_tensor(
+                out=q_grouped[:],
+                in0=live["scaled", n][:].rearrange("p c t -> p t c"),
+                in1=live["spread", n][:].unsqueeze(2).to_broadcast([P, BLOCK, PACK]),
+                op=ALU.mult,
+            )
+            q_codes = stage.tile([P, BLOCK], U32, align_bytes=64)
+            q_scales = stage.tile([P, BLOCK], U8, align_bytes=64)
+            nc.vector.quantize_mx(
+                out=q_codes[:].bitcast(FP8X4), scales=q_scales[:], in_=q_grouped[:].rearrange("p t c -> p (t c)")
+            )
+            live["q_mx", n] = (q_codes, q_scales)
+
+        def score(n):
+            b = n // BLOCKS_PER_BATCH
+            q_codes, q_scales = live["q_mx", n]
+            banks = []
+            for first in range(0, BLOCK_TILES, PAIR):
+                s_ps = psum_ring.tile([P, PAIR, KEYS], F32, tag="bank")
+                for j in range(PAIR):
+                    i = first + j
+                    nc.tensor.matmul_mx(
+                        out=s_ps[:, j, :],
+                        lhsT=q_codes[:, i * P : (i + 1) * P].bitcast(FP8X4),
+                        lhsT_scale=q_scales[:, i * P : (i + 1) * P],
+                        rhs=k_codes[:, b, :].bitcast(FP8X4),
+                        rhs_scale=k_scales[:, b, :],
+                        start=True,
+                        stop=True,
+                    )
+                banks.append(s_ps)
+            live["s", n] = banks
+
+        def store(n):
+            b, half = divmod(n, BLOCKS_PER_BATCH)
+            scores = deep.tile([P, BLOCK_TILES, KEYS], F32)
+            for g in range(BLOCK_TILES // PAIR):
+                nc.vector.tensor_scalar(
+                    out=scores[:, g * PAIR : (g + 1) * PAIR, :],
+                    in0=live["s", n][g][:],
+                    scalar1=1.0 / math.sqrt(D),
+                    scalar2=None,
+                    op0=ALU.mult,
+                )
+            nc.sync.dma_start(
+                out=out[b].rearrange("(p i) s -> p i s", i=TILES_PER_BATCH)[
+                    :, half * BLOCK_TILES : (half + 1) * BLOCK_TILES, :
+                ],
+                in_=scores[:],
+            )
+
+        def run(stage_of_block, n):
+            if 0 <= n < N_BLOCKS:
+                stage_of_block(n)
+
+        for n in range(-2, N_BLOCKS + 2):
+            run(spread_inverse, n)
+            run(scale_on_vector, n + 1)
+            run(store, n - 2)
+            run(scale_on_scalar, n + 1)
+            run(project, n + 2)
+            run(square, n + 2)
+            run(root_mean_square, n + 1)
+            run(score, n - 1)
+            run(normalise, n)

@@ -197,8 +197,12 @@ def tile_crossattention_pb_t_kernel(tc, text, Wq_w, Wq_b, qn_w, k_norm, out):
             nc.vector.reciprocal(out=rstd[:], in_=live["rms", n][:])
             spread = psum_one.tile([P, BLOCK], F32)
             for i in range(BLOCK_TILES):
-                nc.tensor.transpose(
-                    spread[:, i * P : (i + 1) * P], rstd[:, i : i + 1].to_broadcast([P, P]), ident[:]
+                nc.tensor.matmul(
+                    out=spread[:, i * P : (i + 1) * P],
+                    lhsT=rstd[:, i : i + 1].to_broadcast([P, P]),
+                    rhs=ident[:],
+                    start=True,
+                    stop=True,
                 )
             live["spread", n] = spread
 

@@ -40,6 +40,7 @@ def tile_crossattention_pb_t_kernel(tc, text, Wq_w, Wq_b, qn_w, k_norm, out):
         raw = ctx.enter_context(tc.tile_pool(name="raw", bufs=4))
         stage = ctx.enter_context(tc.tile_pool(name="stage", bufs=2))
         deep = ctx.enter_context(tc.tile_pool(name="deep", bufs=3))
+        deeper = ctx.enter_context(tc.tile_pool(name="deeper", bufs=4))
         psum_ring = ctx.enter_context(tc.psum_pool(name="psum_ring", bufs=6))
         psum_one = ctx.enter_context(tc.psum_pool(name="psum_one", bufs=1))
 
@@ -71,6 +72,16 @@ def tile_crossattention_pb_t_kernel(tc, text, Wq_w, Wq_b, qn_w, k_norm, out):
         nc.vector.tensor_copy(out=gain[:], in_=gain_bf[:])
         nc.vector.tensor_tensor(out=gain_bias[:], in0=gain[:], in1=bias[:], op=ALU.mult)
 
+        turned_operands = []
+
+        def quantise(operand):
+            grouped, codes, scales = operand
+            nc.vector.quantize_mx(
+                out=codes.bitcast(FP8X4),
+                scales=scales,
+                in_=grouped[:].rearrange("p r t -> p (r t)"),
+            )
+
         def transpose_and_quantise(rows, n_tiles, codes, scales):
             words = rows.bitcast(F32)
             grouped = deep.tile([P, n_tiles * P, PACK], BF16, align_bytes=64, tag="grouped%d" % n_tiles)
@@ -84,21 +95,13 @@ def tile_crossattention_pb_t_kernel(tc, text, Wq_w, Wq_b, qn_w, k_norm, out):
                             words[:, first + j, u * P : (u + 1) * P],
                             ident[:],
                         )
-                if (first // PAIR) % 2 == 0:
-                    nc.vector.tensor_copy(
-                        out=grouped_words[:, first * P : (first + PAIR) * P, :],
-                        in_=turned[:].rearrange("p u r -> p r u"),
-                    )
-                else:
-                    nc.scalar.copy(
-                        out=grouped_words[:, first * P : (first + PAIR) * P, :],
-                        in_=turned[:].rearrange("p u r -> p r u"),
-                    )
-            nc.vector.quantize_mx(
-                out=codes.bitcast(FP8X4),
-                scales=scales,
-                in_=grouped[:].rearrange("p r t -> p (r t)"),
-            )
+                nc.scalar.copy(
+                    out=grouped_words[:, first * P : (first + PAIR) * P, :],
+                    in_=turned[:].rearrange("p u r -> p r u"),
+                )
+            turned_operands.append((grouped, codes, scales))
+            if len(turned_operands) > 1:
+                quantise(turned_operands[-2])
 
         w_codes = const.tile([P, D], U32, align_bytes=64)
         w_scales = const.tile([P, D], U8, align_bytes=64)
@@ -122,6 +125,7 @@ def tile_crossattention_pb_t_kernel(tc, text, Wq_w, Wq_b, qn_w, k_norm, out):
                     x_scales[:, n, :],
                 )
             transpose_and_quantise(k_raw[:], KEY_TILES, k_codes[:, b, :], k_scales[:, b, :])
+        quantise(turned_operands[-1])
 
         live = {}
 
@@ -155,18 +159,18 @@ def tile_crossattention_pb_t_kernel(tc, text, Wq_w, Wq_b, qn_w, k_norm, out):
             live["halves", n] = halves
 
         def scale_on_vector(n):
-            scaled = deep.tile([P, CHUNKS, BLOCK], F32)
             nc.vector.tensor_scalar(
-                out=scaled[:, CHUNKS - 1, :],
+                out=live["scaled", n][:, CHUNKS - 1, :],
                 in0=live["q", n][CHUNKS - 1][:],
                 scalar1=gain[:, CHUNKS - 1 : CHUNKS],
                 scalar2=gain_bias[:, CHUNKS - 1 : CHUNKS],
                 op0=ALU.mult,
                 op1=ALU.add,
             )
-            live["scaled", n] = scaled
 
         def scale_on_scalar(n):
+            scaled = deeper.tile([P, CHUNKS, BLOCK], F32)
+            live["scaled", n] = scaled
             for c in range(CHUNKS - 1):
                 nc.scalar.activation(
                     out=live["scaled", n][:, c, :],
@@ -192,17 +196,16 @@ def tile_crossattention_pb_t_kernel(tc, text, Wq_w, Wq_b, qn_w, k_norm, out):
             nc.scalar.activation(out=rms[:], in_=sums[:], func=ACT.Sqrt, bias=eps[:], scale=1.0 / D)
             live["rms", n] = rms
 
-        def spread_inverse(n):
-            rstd = stage.tile([P, BLOCK_TILES], F32)
+        def invert(n):
+            rstd = deep.tile([P, BLOCK_TILES], F32)
             nc.vector.reciprocal(out=rstd[:], in_=live["rms", n][:])
+            live["rstd", n] = rstd
+
+        def spread_inverse(n):
             spread = psum_one.tile([P, BLOCK], F32)
             for i in range(BLOCK_TILES):
-                nc.tensor.matmul(
-                    out=spread[:, i * P : (i + 1) * P],
-                    lhsT=rstd[:, i : i + 1].to_broadcast([P, P]),
-                    rhs=ident[:],
-                    start=True,
-                    stop=True,
+                nc.tensor.transpose(
+                    spread[:, i * P : (i + 1) * P], live["rstd", n][:, i : i + 1].to_broadcast([P, P]), ident[:]
                 )
             live["spread", n] = spread
 
@@ -214,8 +217,8 @@ def tile_crossattention_pb_t_kernel(tc, text, Wq_w, Wq_b, qn_w, k_norm, out):
                 in1=live["spread", n][:].unsqueeze(2).to_broadcast([P, BLOCK, PACK]),
                 op=ALU.mult,
             )
-            q_codes = stage.tile([P, BLOCK], U32, align_bytes=64)
-            q_scales = stage.tile([P, BLOCK], U8, align_bytes=64)
+            q_codes = deep.tile([P, BLOCK], U32, align_bytes=64)
+            q_scales = deep.tile([P, BLOCK], U8, align_bytes=64)
             nc.vector.quantize_mx(
                 out=q_codes[:].bitcast(FP8X4), scales=q_scales[:], in_=q_grouped[:].rearrange("p t c -> p (t c)")
             )
@@ -245,12 +248,8 @@ def tile_crossattention_pb_t_kernel(tc, text, Wq_w, Wq_b, qn_w, k_norm, out):
             b, half = divmod(n, BLOCKS_PER_BATCH)
             scores = deep.tile([P, BLOCK_TILES, KEYS], F32)
             for g in range(BLOCK_TILES // PAIR):
-                nc.vector.tensor_scalar(
-                    out=scores[:, g * PAIR : (g + 1) * PAIR, :],
-                    in0=live["s", n][g][:],
-                    scalar1=1.0 / math.sqrt(D),
-                    scalar2=None,
-                    op0=ALU.mult,
+                nc.scalar.mul(
+                    out=scores[:, g * PAIR : (g + 1) * PAIR, :], in_=live["s", n][g][:], mul=1.0 / math.sqrt(D)
                 )
             nc.sync.dma_start(
                 out=out[b].rearrange("(p i) s -> p i s", i=TILES_PER_BATCH)[
@@ -263,13 +262,14 @@ def tile_crossattention_pb_t_kernel(tc, text, Wq_w, Wq_b, qn_w, k_norm, out):
             if 0 <= n < N_BLOCKS:
                 stage_of_block(n)
 
-        for n in range(-2, N_BLOCKS + 2):
-            run(spread_inverse, n)
-            run(scale_on_vector, n + 1)
-            run(store, n - 2)
+        for n in range(-2, N_BLOCKS + 3):
+            run(spread_inverse, n - 1)
             run(scale_on_scalar, n + 1)
+            run(scale_on_vector, n + 1)
+            run(store, n - 3)
             run(project, n + 2)
+            run(invert, n)
             run(square, n + 2)
             run(root_mean_square, n + 1)
-            run(score, n - 1)
-            run(normalise, n)
+            run(score, n - 2)
+            run(normalise, n - 1)

@@ -28,6 +28,7 @@ BLOCK = BLOCK_TILES * P
 BLOCKS_PER_BATCH = TOKENS // BLOCK
 N_BLOCKS = BATCHES * BLOCKS_PER_BATCH
 PAIR = 2
+RUN = 4
 
 FLOPS = 2 * BATCHES * TOKENS * D * D + 2 * BATCHES * TOKENS * D * KEYS
 
@@ -212,9 +213,12 @@ def tile_crossattention_pb_t_kernel(tc, text, Wq_w, Wq_b, qn_w, k_norm, out):
         def normalise(n):
             q_grouped = stage.tile([P, BLOCK, PACK], BF16, align_bytes=64)
             nc.vector.tensor_tensor(
-                out=q_grouped[:],
-                in0=live["scaled", n][:].rearrange("p c t -> p t c"),
-                in1=live["spread", n][:].unsqueeze(2).to_broadcast([P, BLOCK, PACK]),
+                out=q_grouped[:].rearrange("p (t i) c -> p t c i", i=RUN),
+                in0=live["scaled", n][:].rearrange("p c (t i) -> p t c i", i=RUN),
+                in1=live["spread", n][:]
+                .rearrange("p (t i) -> p t i", i=RUN)
+                .unsqueeze(2)
+                .to_broadcast([P, BLOCK // RUN, PACK, RUN]),
                 op=ALU.mult,
             )
             q_codes = deep.tile([P, BLOCK], U32, align_bytes=64)
@@ -247,10 +251,14 @@ def tile_crossattention_pb_t_kernel(tc, text, Wq_w, Wq_b, qn_w, k_norm, out):
         def store(n):
             b, half = divmod(n, BLOCKS_PER_BATCH)
             scores = deep.tile([P, BLOCK_TILES, KEYS], F32)
-            for g in range(BLOCK_TILES // PAIR):
-                nc.scalar.mul(
-                    out=scores[:, g * PAIR : (g + 1) * PAIR, :], in_=live["s", n][g][:], mul=1.0 / math.sqrt(D)
-                )
+            nc.scalar.mul(out=scores[:, 0:PAIR, :], in_=live["s", n][0][:], mul=1.0 / math.sqrt(D))
+            nc.vector.tensor_scalar(
+                out=scores[:, PAIR : 2 * PAIR, :],
+                in0=live["s", n][1][:],
+                scalar1=1.0 / math.sqrt(D),
+                scalar2=None,
+                op0=ALU.mult,
+            )
             nc.sync.dma_start(
                 out=out[b].rearrange("(p i) s -> p i s", i=TILES_PER_BATCH)[
                     :, half * BLOCK_TILES : (half + 1) * BLOCK_TILES, :

@@ -181,7 +181,7 @@ def tile_crossattention_pb_t_kernel(tc, text, Wq_w, Wq_b, qn_w, k_norm, out):
                     scale=gain[:, c : c + 1],
                 )
 
-        def root_mean_square(n):
+        def inverse_rms(n):
             halves = live["halves", n]
             sums = psum_one.tile([P, BLOCK_TILES], F32)
             for i in range(BLOCK_TILES):
@@ -193,13 +193,8 @@ def tile_crossattention_pb_t_kernel(tc, text, Wq_w, Wq_b, qn_w, k_norm, out):
                         start=(h == 0),
                         stop=(h == 1),
                     )
-            rms = stage.tile([P, BLOCK_TILES], F32)
-            nc.scalar.activation(out=rms[:], in_=sums[:], func=ACT.Sqrt, bias=eps[:], scale=1.0 / D)
-            live["rms", n] = rms
-
-        def invert(n):
             rstd = deep.tile([P, BLOCK_TILES], F32)
-            nc.vector.reciprocal(out=rstd[:], in_=live["rms", n][:])
+            nc.scalar.activation(out=rstd[:], in_=sums[:], func=ACT.Abs_reciprocal_sqrt, bias=eps[:], scale=1.0 / D)
             live["rstd", n] = rstd
 
         def spread_inverse(n):
@@ -270,14 +265,13 @@ def tile_crossattention_pb_t_kernel(tc, text, Wq_w, Wq_b, qn_w, k_norm, out):
             if 0 <= n < N_BLOCKS:
                 stage_of_block(n)
 
-        for n in range(-2, N_BLOCKS + 3):
-            run(spread_inverse, n - 1)
+        for n in range(-2, N_BLOCKS + 2):
+            run(spread_inverse, n)
             run(scale_on_scalar, n + 1)
             run(scale_on_vector, n + 1)
-            run(store, n - 3)
+            run(store, n - 2)
             run(project, n + 2)
-            run(invert, n)
             run(square, n + 2)
-            run(root_mean_square, n + 1)
-            run(score, n - 2)
-            run(normalise, n - 1)
+            run(inverse_rms, n + 1)
+            run(score, n - 1)
+            run(normalise, n)

from contextlib import ExitStack
import math

import concourse.mybir as mybir
from concourse.masks import make_identity

F32 = mybir.dt.float32
BF16 = mybir.dt.bfloat16
U32 = mybir.dt.uint32
U8 = mybir.dt.uint8
FP8X4 = mybir.dt.float8_e4m3fn_x4
ACT = mybir.ActivationFunctionType
ALU = mybir.AluOpType

P = 128
PACK = 4
BATCHES = 8
TOKENS = 1024
KEYS = 256
D = 512
EPS = 1e-6

CHUNKS = D // P
TILES_PER_BATCH = TOKENS // P
KEY_TILES = KEYS // P
BLOCK_TILES = 4
BLOCK = BLOCK_TILES * P
BLOCKS_PER_BATCH = TOKENS // BLOCK
N_BLOCKS = BATCHES * BLOCKS_PER_BATCH
PAIR = 2
RUN = 4

FLOPS = 2 * BATCHES * TOKENS * D * D + 2 * BATCHES * TOKENS * D * KEYS


def tile_crossattention_pb_t_kernel(tc, text, Wq_w, Wq_b, qn_w, k_norm, out):
    nc = tc.nc
    with ExitStack() as ctx:
        ctx.enter_context(tc.manual_schedule())
        const = ctx.enter_context(tc.tile_pool(name="const", bufs=1))
        raw = ctx.enter_context(tc.tile_pool(name="raw", bufs=4))
        stage = ctx.enter_context(tc.tile_pool(name="stage", bufs=2))
        deep = ctx.enter_context(tc.tile_pool(name="deep", bufs=3))
        deeper = ctx.enter_context(tc.tile_pool(name="deeper", bufs=4))
        psum_ring = ctx.enter_context(tc.psum_pool(name="psum_ring", bufs=6))
        psum_one = ctx.enter_context(tc.psum_pool(name="psum_one", bufs=1))

        w_raw = const.tile([P, CHUNKS, D], BF16)
        nc.sync.dma_start(
            out=w_raw[:].rearrange("p (u e) k -> p u e k", e=2),
            in_=Wq_w.rearrange("(u p e) k -> p u e k", u=2, e=2),
        )
        bias_bf = const.tile([P, CHUNKS], BF16)
        gain_bf = const.tile([P, CHUNKS], BF16)
        nc.scalar.dma_start(
            out=bias_bf[:].rearrange("p (u e) -> p u e", e=2),
            in_=Wq_b.rearrange("(u p e) -> p u e", u=2, e=2),
        )
        nc.scalar.dma_start(
            out=gain_bf[:].rearrange("p (u e) -> p u e", e=2),
            in_=qn_w.rearrange("(u p e) -> p u e", u=2, e=2),
        )
        ident = const.tile([P, P], F32)
        make_identity(nc, ident[:])
        ones = const.tile([P, 1], F32)
        nc.vector.memset(ones[:], 1.0)
        eps = const.tile([P, 1], F32)
        nc.vector.memset(eps[:], EPS)
        bias = const.tile([P, CHUNKS], F32)
        gain = const.tile([P, CHUNKS], F32)
        gain_bias = const.tile([P, CHUNKS], F32)
        nc.vector.tensor_copy(out=bias[:], in_=bias_bf[:])
        nc.vector.tensor_copy(out=gain[:], in_=gain_bf[:])
        nc.vector.tensor_tensor(out=gain_bias[:], in0=gain[:], in1=bias[:], op=ALU.mult)

        turned_operands = []

        def quantise(operand):
            grouped, codes, scales = operand
            nc.vector.quantize_mx(
                out=codes.bitcast(FP8X4),
                scales=scales,
                in_=grouped[:].rearrange("p r t -> p (r t)"),
            )

        def transpose_and_quantise(rows, n_tiles, codes, scales):
            words = rows.bitcast(F32)
            grouped = deep.tile([P, n_tiles * P, PACK], BF16, align_bytes=64, tag="grouped%d" % n_tiles)
            grouped_words = grouped[:].bitcast(F32)
            for first in range(0, n_tiles, PAIR):
                turned = psum_ring.tile([P, 2, PAIR * P], F32, tag="bank")
                for j in range(PAIR):
                    for u in range(2):
                        nc.tensor.transpose(
                            turned[:, u, j * P : (j + 1) * P],
                            words[:, first + j, u * P : (u + 1) * P],
                            ident[:],
                        )
                nc.scalar.copy(
                    out=grouped_words[:, first * P : (first + PAIR) * P, :],
                    in_=turned[:].rearrange("p u r -> p r u"),
                )
            turned_operands.append((grouped, codes, scales))
            if len(turned_operands) > 1:
                quantise(turned_operands[-2])

        w_codes = const.tile([P, D], U32, align_bytes=64)
        w_scales = const.tile([P, D], U8, align_bytes=64)
        x_codes = const.tile([P, N_BLOCKS, BLOCK], U32, align_bytes=64)
        x_scales = const.tile([P, N_BLOCKS, BLOCK], U8, align_bytes=64)
        k_codes = const.tile([P, BATCHES, KEYS], U32, align_bytes=64)
        k_scales = const.tile([P, BATCHES, KEYS], U8, align_bytes=64)

        transpose_and_quantise(w_raw[:], CHUNKS, w_codes[:], w_scales[:])
        for b in range(BATCHES):
            text_raw = raw.tile([P, TILES_PER_BATCH, D], BF16)
            nc.sync.dma_start(out=text_raw[:], in_=text[b].rearrange("(p i) k -> p i k", i=TILES_PER_BATCH))
            k_raw = raw.tile([P, KEY_TILES, D], BF16)
            nc.sync.dma_start(out=k_raw[:], in_=k_norm[b].rearrange("(j p) d -> p j d", p=P))
            for half in range(BLOCKS_PER_BATCH):
                n = b * BLOCKS_PER_BATCH + half
                transpose_and_quantise(
                    text_raw[:, half * BLOCK_TILES : (half + 1) * BLOCK_TILES, :],
                    BLOCK_TILES,
                    x_codes[:, n, :],
                    x_scales[:, n, :],
                )
            transpose_and_quantise(k_raw[:], KEY_TILES, k_codes[:, b, :], k_scales[:, b, :])
        quantise(turned_operands[-1])

        live = {}

        def project(n):
            banks = []
            for c in range(CHUNKS):
                q_ps = psum_ring.tile([P, BLOCK], F32, tag="bank")
                nc.tensor.matmul_mx(
                    out=q_ps[:],
                    lhsT=w_codes[:, c * P : (c + 1) * P].bitcast(FP8X4),
                    lhsT_scale=w_scales[:, c * P : (c + 1) * P],
                    rhs=x_codes[:, n, :].bitcast(FP8X4),
                    rhs_scale=x_scales[:, n, :],
                    start=True,
                    stop=True,
                )
                banks.append(q_ps)
            live["q", n] = banks

        def square(n):
            squares = stage.tile([P, CHUNKS, BLOCK], F32)
            halves = deep.tile([P, 2, BLOCK], F32)
            for c in range(CHUNKS):
                nc.scalar.activation(
                    out=squares[:, c, :], in_=live["q", n][c][:], func=ACT.Square, bias=bias[:, c : c + 1], scale=1.0
                )
            for h in range(2):
                nc.gpsimd.tensor_tensor(
                    out=halves[:, h, :], in0=squares[:, 2 * h, :], in1=squares[:, 2 * h + 1, :], op=ALU.add
                )
            live["halves", n] = halves

        def scale_on_vector(n):
            nc.vector.tensor_scalar(
                out=live["scaled", n][:, CHUNKS - 1, :],
                in0=live["q", n][CHUNKS - 1][:],
                scalar1=gain[:, CHUNKS - 1 : CHUNKS],
                scalar2=gain_bias[:, CHUNKS - 1 : CHUNKS],
                op0=ALU.mult,
                op1=ALU.add,
            )

        def scale_on_scalar(n):
            scaled = deeper.tile([P, CHUNKS, BLOCK], F32)
            live["scaled", n] = scaled
            for c in range(CHUNKS - 1):
                nc.scalar.activation(
                    out=live["scaled", n][:, c, :],
                    in_=live["q", n][c][:],
                    func=ACT.Identity,
                    bias=gain_bias[:, c : c + 1],
                    scale=gain[:, c : c + 1],
                )

        def inverse_rms(n):
            halves = live["halves", n]
            sums = psum_one.tile([P, BLOCK_TILES], F32)
            for i in range(BLOCK_TILES):
                for h in range(2):
                    nc.tensor.matmul(
                        out=sums[:, i : i + 1],
                        lhsT=halves[:, h, i * P : (i + 1) * P],
                        rhs=ones[:],
                        start=(h == 0),
                        stop=(h == 1),
                    )
            rstd = deep.tile([P, BLOCK_TILES], F32)
            nc.scalar.activation(out=rstd[:], in_=sums[:], func=ACT.Abs_reciprocal_sqrt, bias=eps[:], scale=1.0 / D)
            live["rstd", n] = rstd

        def spread_inverse(n):
            spread = psum_one.tile([P, BLOCK], F32)
            for i in range(BLOCK_TILES):
                nc.tensor.transpose(
                    spread[:, i * P : (i + 1) * P], live["rstd", n][:, i : i + 1].to_broadcast([P, P]), ident[:]
                )
            live["spread", n] = spread

        def normalise(n):
            q_grouped = stage.tile([P, BLOCK, PACK], BF16, align_bytes=64)
            nc.vector.tensor_tensor(
                out=q_grouped[:].rearrange("p (t i) c -> p t c i", i=RUN),
                in0=live["scaled", n][:].rearrange("p c (t i) -> p t c i", i=RUN),
                in1=live["spread", n][:]
                .rearrange("p (t i) -> p t i", i=RUN)
                .unsqueeze(2)
                .to_broadcast([P, BLOCK // RUN, PACK, RUN]),
                op=ALU.mult,
            )
            q_codes = deep.tile([P, BLOCK], U32, align_bytes=64)
            q_scales = deep.tile([P, BLOCK], U8, align_bytes=64)
            nc.vector.quantize_mx(
                out=q_codes[:].bitcast(FP8X4), scales=q_scales[:], in_=q_grouped[:].rearrange("p t c -> p (t c)")
            )
            live["q_mx", n] = (q_codes, q_scales)

        def score(n):
            b = n // BLOCKS_PER_BATCH
            q_codes, q_scales = live["q_mx", n]
            banks = []
            for first in range(0, BLOCK_TILES, PAIR):
                s_ps = psum_ring.tile([P, PAIR, KEYS], F32, tag="bank")
                for j in range(PAIR):
                    i = first + j
                    nc.tensor.matmul_mx(
                        out=s_ps[:, j, :],
                        lhsT=q_codes[:, i * P : (i + 1) * P].bitcast(FP8X4),
                        lhsT_scale=q_scales[:, i * P : (i + 1) * P],
                        rhs=k_codes[:, b, :].bitcast(FP8X4),
                        rhs_scale=k_scales[:, b, :],
                        start=True,
                        stop=True,
                    )
                banks.append(s_ps)
            live["s", n] = banks

        def store(n):
            b, half = divmod(n, BLOCKS_PER_BATCH)
            scores = deep.tile([P, BLOCK_TILES, KEYS], F32)
            nc.scalar.mul(out=scores[:, 0:PAIR, :], in_=live["s", n][0][:], mul=1.0 / math.sqrt(D))
            nc.vector.tensor_scalar(
                out=scores[:, PAIR : 2 * PAIR, :],
                in0=live["s", n][1][:],
                scalar1=1.0 / math.sqrt(D),
                scalar2=None,
                op0=ALU.mult,
            )
            nc.sync.dma_start(
                out=out[b].rearrange("(p i) s -> p i s", i=TILES_PER_BATCH)[
                    :, half * BLOCK_TILES : (half + 1) * BLOCK_TILES, :
                ],
                in_=scores[:],
            )

        def run(stage_of_block, n):
            if 0 <= n < N_BLOCKS:
                stage_of_block(n)

        for n in range(-2, N_BLOCKS + 2):
            run(spread_inverse, n)
            run(scale_on_scalar, n + 1)
            run(scale_on_vector, n + 1)
            run(store, n - 2)
            run(project, n + 2)
            run(square, n + 2)
            run(inverse_rms, n + 1)
            run(score, n - 1)
            run(normalise, n)
